import numpy as np
import ml_dtypes


def mxq(x, axis, fmt="e4m3"):
    dtype, down = {"e4m3": (ml_dtypes.float8_e4m3fn, 7), "e5m2": (ml_dtypes.float8_e5m2, 14)}[fmt]
    v = np.moveaxis(np.asarray(x, np.float32).astype(ml_dtypes.bfloat16).astype(np.float64), axis, -1)
    blocks = v.reshape(v.shape[:-1] + (-1, 32))
    amax = np.abs(blocks).max(-1, keepdims=True)
    byte = np.maximum(np.where(amax > 0, np.frexp(amax)[1] - 1 + 127, 0) - down, 1)
    scale = np.exp2(byte - 127.0)
    codes = (blocks / scale).astype(np.float32).astype(dtype).astype(np.float64)
    return np.moveaxis((codes * scale).reshape(v.shape), -1, axis)


WIDE = False


def mx_kscale(k):
    if not WIDE:
        return np.ones(k)
    levels = np.array([10, -10, 5, -5, 0])
    if k % 512:
        return np.exp2(np.random.permutation(np.resize(levels, k // 32))).repeat(32)
    a = np.empty((k // 512, 16))
    for p in range(k // 512):
        a[p, :8] = np.random.permutation(np.resize(levels, 8))
        for g in range(8):
            far = levels[np.abs(levels - a[p, g]) >= 10]
            a[p, g + 8] = far[np.random.randint(len(far))]
    return np.exp2(a.ravel()).repeat(32)


BF16 = ml_dtypes.bfloat16


def bf(x):
    return np.asarray(x, np.float32).astype(BF16)


def f64(x):
    return np.asarray(x).astype(np.float64)


B, C, C8, H, W, S = 1, 512, 128, 64, 64, 32
T = H * W
S2 = S * S
PH, PW = H // S, W // S


def draw0():
    s = mx_kscale(C)
    return {"x": bf(np.random.standard_normal((B, C, H, W)) * s[None, :, None, None]),
            "Wq": bf(np.random.standard_normal((C8, C)) * 2.0 / np.sqrt(C) / s[None, :]),
            "bq": bf(np.random.standard_normal(C8) * 0.5),
            "Wk": bf(np.random.standard_normal((C8, C)) * 2.0 / np.sqrt(C) / s[None, :]),
            "bk": bf(np.random.standard_normal(C8) * 0.3)}


def core(x, Wq, bq, Wk, bk):
    xq = mxq(f64(x).reshape(B, C, T), 1, "e4m3")
    qc = (mxq(f64(Wq), 1, "e4m3") @ xq) + f64(bq)[None, :, None]
    kc = (mxq(f64(Wk), 1, "e4m3") @ xq) + f64(bk)[None, :, None]
    q = qc.transpose(0, 2, 1)
    k_pool = kc.reshape(B, C8, S, PH, S, PW).mean(axis=(3, 5)).reshape(B, C8, S2)
    return q, k_pool


def e4m3fn_bytes(y):
    return np.clip(np.asarray(y, np.float64), -448.0, 448.0).astype(np.float32).astype(ml_dtypes.float8_e4m3fn).view(np.uint8)


def e4m3fn_values(b):
    return np.asarray(b, np.uint8).view(ml_dtypes.float8_e4m3fn).astype(np.float64)


def setup_inputs():
    d = draw0()
    x0 = np.asarray(d['x']).astype(np.float64)
    s = (np.max(np.abs(x0), axis=(0, 2, 3), keepdims=True) / 448.0).astype(np.float32)
    out = {}
    for k, v in d.items():
        if k == 'x':
            out['x_bytes'] = e4m3fn_bytes(x0 / s.astype(np.float64))
            out['x_scale'] = s
        else:
            out[k] = v
    return out


def reference(x_bytes, x_scale, Wq, bq, Wk, bk):
    return core(e4m3fn_values(x_bytes) * x_scale.astype(np.float64), Wq, bq, Wk, bk)

@@ -1,0 +1,202 @@
+from contextlib import ExitStack
+
+import concourse.mybir as mybir
+from concourse.masks import make_identity
+
+F32 = mybir.dt.float32
+BF16 = mybir.dt.bfloat16
+U32 = mybir.dt.uint32
+U8 = mybir.dt.uint8
+FP8 = mybir.dt.float8_e4m3fn
+FP8X4 = mybir.dt.float8_e4m3fn_x4
+ACT = mybir.ActivationFunctionType
+ALU = mybir.AluOpType
+
+P = 128
+C = 512
+O = 128
+H = 64
+W = 64
+T = H * W
+FLOPS = 2 * 2 * O * C * T
+
+CHUNK_ROWS = [4, 4, 8, 8, 8, 8, 8, 8, 4, 4]
+LOAD_ROWS = [4, 4, 8, 16, 32]
+VECTOR_WIDENS = {0: (2, 3)}
+
+
+def tile_selfattention_pb_kernel(tc, x_bytes, x_scale, Wq, bq, Wk, bk, out_0, out_1):
+    nc = tc.nc
+    n_chunks = len(CHUNK_ROWS)
+    row0 = [sum(CHUNK_ROWS[:c]) for c in range(n_chunks)]
+    load0 = [sum(LOAD_ROWS[:d]) for d in range(len(LOAD_ROWS))]
+
+    xv = x_bytes.rearrange("b (p t) h w -> p t (b h w)", t=4)
+    q2 = out_0.rearrange("b n o -> (b n) o")
+    k2 = out_1.rearrange("b o n -> (b o) n")
+
+    with ExitStack() as ctx:
+        keep = ctx.enter_context(tc.tile_pool(name="keep", bufs=1))
+        stream = ctx.enter_context(tc.tile_pool(name="stream", bufs=3))
+        psum1 = ctx.enter_context(tc.psum_pool(name="psum1", bufs=1))
+        psumq = ctx.enter_context(tc.psum_pool(name="psumq", bufs=3))
+        psumk = ctx.enter_context(tc.psum_pool(name="psumk", bufs=2))
+
+        xs = keep.tile([P, 4], F32, name="xs")
+        nc.scalar.dma_start(out=xs[:], in_=x_scale.rearrange("a (p t) b c -> p (a t b c)", t=4))
+        xb = []
+        wraw = keep.tile([P, 2, C], BF16, name="wraw")
+        for d in range(len(LOAD_ROWS)):
+            n_px = LOAD_ROWS[d] * W
+            xbytes = keep.tile([P, 4, n_px], U8, name="xbytes%d" % d)
+            nc.sync.dma_start(out=xbytes[:], in_=xv[:, :, load0[d] * W : load0[d] * W + n_px])
+            xb.append(xbytes)
+            if d == 1:
+                nc.sync.dma_start(out=wraw[:, 0, :], in_=Wq)
+                nc.sync.dma_start(out=wraw[:, 1, :], in_=Wk)
+        brow = keep.tile([P, O], BF16, name="brow")
+        nc.gpsimd.memset(brow[:], 0.0)
+        nc.scalar.dma_start(out=brow[0:1, :], in_=bq.rearrange("(a o) -> a o", a=1))
+        bkc = keep.tile([P, 1], BF16, name="bkc")
+        nc.scalar.dma_start(out=bkc[:], in_=bk.rearrange("(p a) -> p a", a=1))
+
+        warm = keep.tile([P, 1], F32, name="warm")
+        nc.gpsimd.memset(warm[:], 0.0)
+        warm2 = keep.tile([P, 1], F32, name="warm2")
+        nc.scalar.activation(out=warm2[:], in_=warm[:], func=ACT.Copy)
+        ident = keep.tile([P, P], F32, name="ident")
+        make_identity(nc, ident[:])
+        ones = keep.tile([P, P], BF16, name="ones")
+        nc.gpsimd.memset(ones[:], 1.0)
+
+        state = {}
+
+        def widen(c):
+            rows = CHUNK_ROWS[c]
+            n_px = rows * W
+            d = max(i for i in range(len(LOAD_ROWS)) if load0[i] <= row0[c])
+            off = (row0[c] - load0[d]) * W
+            xw = stream.tile([P, 4, n_px], BF16, name="xw", tag="xw")
+            for t in range(4):
+                src = xb[d][:, t, off : off + n_px].bitcast(FP8)
+                if t in VECTOR_WIDENS.get(c, ()):
+                    nc.vector.tensor_scalar(out=xw[:, t, :], in0=src, scalar1=xs[:, t : t + 1], scalar2=None, op0=ALU.mult)
+                else:
+                    nc.scalar.activation(out=xw[:, t, :], in_=src, func=ACT.Copy, scale=xs[:, t : t + 1])
+            state[("xw", c)] = xw
+
+        def interleave(c):
+            n_px = CHUNK_ROWS[c] * W
+            xw = state[("xw", c)]
+            xg = stream.tile([P, 4 * n_px], BF16, name="xg", tag="xg", align_bytes=64)
+            nc.vector.tensor_copy(
+                out=xg[:].rearrange("p (d c t) -> p d c t", d=2, t=4),
+                in_=xw[:].rearrange("p t (c d) -> p d c t", d=2),
+            )
+            state[("xg", c)] = xg
+
+        def quantize(c):
+            n_px = CHUNK_ROWS[c] * W
+            xc = stream.tile([P, n_px], U32, name="xc", tag="xc", align_bytes=64)
+            xsc = stream.tile([P, n_px], U8, name="xsc", tag="xsc", align_bytes=64)
+            nc.vector.quantize_mx(out=xc[:].bitcast(FP8X4), scales=xsc[:], in_=state[("xg", c)][:])
+            state[("xc", c)] = (xc, xsc)
+
+        def weights_a():
+            wps = psum1.tile([P, 4 * P], F32, name="wps")
+            words = wraw[:].bitcast(F32)
+            for w in range(2):
+                for u in range(2):
+                    nc.tensor.transpose(wps[:, (2 * w + u) * P : (2 * w + u + 1) * P], words[:, w, u : C // 2 : 2], ident[:])
+            wg = keep.tile([P, 2 * O * 4], BF16, name="wg", align_bytes=64)
+            nc.vector.tensor_copy(
+                out=wg[:].bitcast(F32).rearrange("p (w o u) -> p w o u", w=2, u=2),
+                in_=wps[:].rearrange("p (w u o) -> p w o u", w=2, u=2),
+            )
+            state["wg"] = wg
+            bps = psum1.tile([P, O], F32, name="bps")
+            nc.tensor.matmul(bps[:], lhsT=ones[:], rhs=brow[:], start=True, stop=True)
+            bqb = keep.tile([P, O], F32, name="bqb")
+            nc.scalar.copy(out=bqb[:], in_=bps[:])
+            state["bqb"] = bqb
+
+        def weights_b():
+            wc = keep.tile([P, 2 * O], U32, name="wc", align_bytes=64)
+            wsc = keep.tile([P, 2 * O], U8, name="wsc", align_bytes=64)
+            nc.vector.quantize_mx(out=wc[:].bitcast(FP8X4), scales=wsc[:], in_=state["wg"][:])
+            state["wc"] = (wc, wsc)
+
+        def multiply(c):
+            rows = CHUNK_ROWS[c]
+            xc, xsc = state[("xc", c)]
+            wc, wsc = state["wc"]
+            n_ih = rows // 4
+            qps = psumq.tile([P, 4 * O], F32, name="qps", tag="qps")
+            for dj in range(2):
+                for ih in range(n_ih):
+                    g = dj * n_ih + ih
+                    slot = ih * 2 + dj
+                    nc.tensor.matmul_mx(
+                        out=qps[:, slot * O : (slot + 1) * O],
+                        lhsT=xc[:, g * P : (g + 1) * P].bitcast(FP8X4),
+                        lhsT_scale=xsc[:, g * P : (g + 1) * P],
+                        rhs=wc[:, 0:O].bitcast(FP8X4),
+                        rhs_scale=wsc[:, 0:O],
+                        start=True,
+                        stop=True,
+                    )
+            n_k = rows * 32
+            kps = psumk.tile([P, 256], F32, name="kps", tag="kps")
+            for dj in range(2):
+                nc.tensor.matmul_mx(
+                    out=kps[:, 0:n_k],
+                    lhsT=wc[:, O : 2 * O].bitcast(FP8X4),
+                    lhsT_scale=wsc[:, O : 2 * O],
+                    rhs=xc[:, dj * n_k : (dj + 1) * n_k].bitcast(FP8X4),
+                    rhs_scale=xsc[:, dj * n_k : (dj + 1) * n_k],
+                    start=(dj == 0),
+                    stop=(dj == 1),
+                )
+            state[("ps", c)] = (qps, kps)
+
+        def finish(c):
+            rows = CHUNK_ROWS[c]
+            qps, kps = state[("ps", c)]
+            n_g = rows // 2
+            n_m = rows // 2
+            kv = kps[:, 0 : rows * 32].rearrange("p (m e n) -> p m e n", e=2, n=32)
+            ktmp = stream.tile([P, n_m, 32], F32, name="ktmp", tag="ktmp")
+            nc.scalar.activation(out=ktmp[:], in_=kv[:, :, 0, :], func=ACT.Identity, bias=bkc[:], scale=0.25)
+            qsb = stream.tile([P, n_g, O], F32, name="qsb", tag="qsb")
+            nc.vector.tensor_tensor(
+                out=qsb[:],
+                in0=qps[:, 0 : n_g * O].rearrange("p (g o) -> p g o", o=O),
+                in1=state["bqb"][:].unsqueeze(1).to_broadcast([P, n_g, O]),
+                op=ALU.add,
+            )
+            nc.sync.dma_start(
+                out=q2[row0[c] * W : (row0[c] + rows) * W, :].rearrange("(i p d) o -> p i (d o)", p=P, d=2),
+                in_=qsb[:].rearrange("p (i d) o -> p i (d o)", d=2),
+            )
+            ksb = stream.tile([P, n_m, 32], F32, name="ksb", tag="ksb")
+            nc.vector.scalar_tensor_tensor(out=ksb[:], in0=kv[:, :, 1, :], scalar=0.25, in1=ktmp[:], op0=ALU.mult, op1=ALU.add)
+            nc.sync.dma_start(
+                out=k2[:, row0[c] * 16 : (row0[c] + rows) * 16],
+                in_=ksb[:].rearrange("p m n -> p (m n)"),
+            )
+
+        widen(0)
+        for s in range(n_chunks + 2):
+            if s + 1 < n_chunks:
+                widen(s + 1)
+            if s < n_chunks:
+                interleave(s)
+            if s == 0:
+                weights_a()
+            if s == 1:
+                weights_b()
+            if 0 <= s - 1 < n_chunks:
+                quantize(s - 1)
+                multiply(s - 1)
+            if 0 <= s - 2 < n_chunks:
+                finish(s - 2)

@@ -20,9 +20,15 @@ W = 64
 T = H * W
 FLOPS = 2 * 2 * O * C * T
 
-CHUNK_ROWS = [4, 4, 8, 8, 8, 8, 8, 8, 4, 4]
-LOAD_ROWS = [4, 4, 8, 16, 32]
-VECTOR_WIDENS = {0: (2, 3)}
+CHUNK_ROWS = [4, 8, 8, 8, 8, 8, 8, 8, 4]
+LOAD_ROWS = [4, 8, 8, 16, 28]
+K_GROUPS = [[0, 1], [2, 3], [4, 5], [6, 7], [8]]
+VECTOR_WIDENS = {0: (2, 3), 1: (2, 3), 2: (3,), 3: (3,), 4: (3,), 8: (3,)}
+SCALAR_INTERLEAVES = {1: (1,), 7: (1,), 8: (1,)}
+GPSIMD_COLUMNS = {}
+S_LEAD = 2
+K_LAG = 2
+RUN = 1
 
 
 def tile_selfattention_pb_kernel(tc, x_bytes, x_scale, Wq, bq, Wk, bk, out_0, out_1):
@@ -30,6 +36,10 @@ def tile_selfattention_pb_kernel(tc, x_bytes, x_scale, Wq, bq, Wk, bk, out_0, ou
     n_chunks = len(CHUNK_ROWS)
     row0 = [sum(CHUNK_ROWS[:c]) for c in range(n_chunks)]
     load0 = [sum(LOAD_ROWS[:d]) for d in range(len(LOAD_ROWS))]
+    group_of = {}
+    for gi in range(len(K_GROUPS)):
+        for c in K_GROUPS[gi]:
+            group_of[c] = gi
 
     xv = x_bytes.rearrange("b (p t) h w -> p t (b h w)", t=4)
     q2 = out_0.rearrange("b n o -> (b n) o")
@@ -37,10 +47,14 @@ def tile_selfattention_pb_kernel(tc, x_bytes, x_scale, Wq, bq, Wk, bk, out_0, ou
 
     with ExitStack() as ctx:
         keep = ctx.enter_context(tc.tile_pool(name="keep", bufs=1))
-        stream = ctx.enter_context(tc.tile_pool(name="stream", bufs=3))
+        planes = ctx.enter_context(tc.tile_pool(name="planes", bufs=4))
+        grouped = ctx.enter_context(tc.tile_pool(name="grouped", bufs=3))
+        codes = ctx.enter_context(tc.tile_pool(name="codes", bufs=3))
+        outs = ctx.enter_context(tc.tile_pool(name="outs", bufs=4))
         psum1 = ctx.enter_context(tc.psum_pool(name="psum1", bufs=1))
-        psumq = ctx.enter_context(tc.psum_pool(name="psumq", bufs=3))
+        psumq = ctx.enter_context(tc.psum_pool(name="psumq", bufs=4))
         psumk = ctx.enter_context(tc.psum_pool(name="psumk", bufs=2))
+        ctx.enter_context(tc.manual_schedule())
 
         xs = keep.tile([P, 4], F32, name="xs")
         nc.scalar.dma_start(out=xs[:], in_=x_scale.rearrange("a (p t) b c -> p (a t b c)", t=4))
@@ -54,16 +68,15 @@ def tile_selfattention_pb_kernel(tc, x_bytes, x_scale, Wq, bq, Wk, bk, out_0, ou
             if d == 1:
                 nc.sync.dma_start(out=wraw[:, 0, :], in_=Wq)
                 nc.sync.dma_start(out=wraw[:, 1, :], in_=Wk)
+        warm = keep.tile([P, 1], F32, name="warm")
+        nc.gpsimd.memset(warm[:], 0.0)
         brow = keep.tile([P, O], BF16, name="brow")
         nc.gpsimd.memset(brow[:], 0.0)
+        warm2 = keep.tile([P, 1], F32, name="warm2")
+        nc.scalar.activation(out=warm2[:], in_=warm[:], func=ACT.Copy)
         nc.scalar.dma_start(out=brow[0:1, :], in_=bq.rearrange("(a o) -> a o", a=1))
         bkc = keep.tile([P, 1], BF16, name="bkc")
         nc.scalar.dma_start(out=bkc[:], in_=bk.rearrange("(p a) -> p a", a=1))
-
-        warm = keep.tile([P, 1], F32, name="warm")
-        nc.gpsimd.memset(warm[:], 0.0)
-        warm2 = keep.tile([P, 1], F32, name="warm2")
-        nc.scalar.activation(out=warm2[:], in_=warm[:], func=ACT.Copy)
         ident = keep.tile([P, P], F32, name="ident")
         make_identity(nc, ident[:])
         ones = keep.tile([P, P], BF16, name="ones")
@@ -71,34 +84,65 @@ def tile_selfattention_pb_kernel(tc, x_bytes, x_scale, Wq, bq, Wk, bk, out_0, ou
 
         state = {}
 
-        def widen(c):
+        def widen(c, on_vector):
             rows = CHUNK_ROWS[c]
             n_px = rows * W
             d = max(i for i in range(len(LOAD_ROWS)) if load0[i] <= row0[c])
             off = (row0[c] - load0[d]) * W
-            xw = stream.tile([P, 4, n_px], BF16, name="xw", tag="xw")
+            assert off + n_px <= LOAD_ROWS[d] * W
+            if ("xw", c) not in state:
+                xw_new = planes.tile([P, 4, n_px], BF16, name="xw", tag="xw")
+                state[("xw", c)] = xw_new
+            xw = state[("xw", c)]
             for t in range(4):
                 src = xb[d][:, t, off : off + n_px].bitcast(FP8)
                 if t in VECTOR_WIDENS.get(c, ()):
-                    nc.vector.tensor_scalar(out=xw[:, t, :], in0=src, scalar1=xs[:, t : t + 1], scalar2=None, op0=ALU.mult)
-                else:
+                    if on_vector:
+                        nc.vector.tensor_scalar(out=xw[:, t, :], in0=src, scalar1=xs[:, t : t + 1], scalar2=None, op0=ALU.mult)
+                elif not on_vector:
                     nc.scalar.activation(out=xw[:, t, :], in_=src, func=ACT.Copy, scale=xs[:, t : t + 1])
-            state[("xw", c)] = xw
+
+        def views(c):
+            xw = state[("xw", c)]
+            xg = state[("xg", c)]
+            if RUN == 1:
+                dst = xg[:].rearrange("p (d c t) -> p d c t", d=2, t=4)
+                src = xw[:].rearrange("p t (c d) -> p d c t", d=2)
+            else:
+                dst = xg[:].rearrange("p (d c i t) -> p d c t i", d=2, t=4, i=RUN)
+                src = xw[:].rearrange("p t (c i d) -> p d c t i", d=2, i=RUN)
+            return dst, src
+
+        def interleave_gpsimd(c):
+            n_px = CHUNK_ROWS[c] * W
+            xg_new = grouped.tile([P, 4 * n_px], BF16, name="xg", tag="xg", align_bytes=64)
+            state[("xg", c)] = xg_new
+            g = GPSIMD_COLUMNS.get(c, 0) // RUN
+            if g > 0:
+                dst, src = views(c)
+                n_c = n_px // 2 // RUN
+                nc.gpsimd.tensor_scalar(
+                    out=dst[:, :, n_c - g : n_c], in0=src[:, :, n_c - g : n_c], scalar1=1.0, scalar2=0.0, op0=ALU.mult, op1=ALU.add
+                )
 
         def interleave(c):
             n_px = CHUNK_ROWS[c] * W
-            xw = state[("xw", c)]
-            xg = stream.tile([P, 4 * n_px], BF16, name="xg", tag="xg", align_bytes=64)
-            nc.vector.tensor_copy(
-                out=xg[:].rearrange("p (d c t) -> p d c t", d=2, t=4),
-                in_=xw[:].rearrange("p t (c d) -> p d c t", d=2),
-            )
-            state[("xg", c)] = xg
+            dst, src = views(c)
+            n_c = n_px // 2 // RUN - GPSIMD_COLUMNS.get(c, 0) // RUN
+            on_scalar = SCALAR_INTERLEAVES.get(c, ())
+            if len(on_scalar) == 0:
+                nc.vector.tensor_copy(out=dst[:, :, 0:n_c], in_=src[:, :, 0:n_c])
+            else:
+                for d in range(2):
+                    if d in on_scalar:
+                        nc.scalar.copy(out=dst[:, d, 0:n_c], in_=src[:, d, 0:n_c])
+                    else:
+                        nc.vector.tensor_copy(out=dst[:, d, 0:n_c], in_=src[:, d, 0:n_c])
 
         def quantize(c):
             n_px = CHUNK_ROWS[c] * W
-            xc = stream.tile([P, n_px], U32, name="xc", tag="xc", align_bytes=64)
-            xsc = stream.tile([P, n_px], U8, name="xsc", tag="xsc", align_bytes=64)
+            xc = codes.tile([P, n_px], U32, name="xc", tag="xc", align_bytes=64)
+            xsc = codes.tile([P, n_px], U8, name="xsc", tag="xsc", align_bytes=64)
             nc.vector.quantize_mx(out=xc[:].bitcast(FP8X4), scales=xsc[:], in_=state[("xg", c)][:])
             state[("xc", c)] = (xc, xsc)
 
@@ -132,8 +176,8 @@ def tile_selfattention_pb_kernel(tc, x_bytes, x_scale, Wq, bq, Wk, bk, out_0, ou
             wc, wsc = state["wc"]
             n_ih = rows // 4
             qps = psumq.tile([P, 4 * O], F32, name="qps", tag="qps")
-            for dj in range(2):
-                for ih in range(n_ih):
+            for ih in range(n_ih):
+                for dj in range(2):
                     g = dj * n_ih + ih
                     slot = ih * 2 + dj
                     nc.tensor.matmul_mx(
@@ -145,11 +189,16 @@ def tile_selfattention_pb_kernel(tc, x_bytes, x_scale, Wq, bq, Wk, bk, out_0, ou
                         start=True,
                         stop=True,
                     )
+            gi = group_of[c]
+            if c == K_GROUPS[gi][0]:
+                kps_new = psumk.tile([P, 512], F32, name="kps", tag="kps")
+                state[("kps", gi)] = kps_new
+            kps = state[("kps", gi)]
+            k0 = (row0[c] - row0[K_GROUPS[gi][0]]) * 32
             n_k = rows * 32
-            kps = psumk.tile([P, 256], F32, name="kps", tag="kps")
             for dj in range(2):
                 nc.tensor.matmul_mx(
-                    out=kps[:, 0:n_k],
+                    out=kps[:, k0 : k0 + n_k],
                     lhsT=wc[:, O : 2 * O].bitcast(FP8X4),
                     lhsT_scale=wsc[:, O : 2 * O],
                     rhs=xc[:, dj * n_k : (dj + 1) * n_k].bitcast(FP8X4),
@@ -157,20 +206,35 @@ def tile_selfattention_pb_kernel(tc, x_bytes, x_scale, Wq, bq, Wk, bk, out_0, ou
                     start=(dj == 0),
                     stop=(dj == 1),
                 )
-            state[("ps", c)] = (qps, kps)
+            state[("qps", c)] = qps
 
-        def finish(c):
-            rows = CHUNK_ROWS[c]
-            qps, kps = state[("ps", c)]
-            n_g = rows // 2
-            n_m = rows // 2
-            kv = kps[:, 0 : rows * 32].rearrange("p (m e n) -> p m e n", e=2, n=32)
-            ktmp = stream.tile([P, n_m, 32], F32, name="ktmp", tag="ktmp")
+        def group_rows(gi):
+            return sum(CHUNK_ROWS[c] for c in K_GROUPS[gi])
+
+        def keys_even(gi):
+            rows = group_rows(gi)
+            kv = state[("kps", gi)][:, 0 : rows * 32].rearrange("p (m e n) -> p m e n", e=2, n=32)
+            ktmp = outs.tile([P, rows // 2, 32], F32, name="ktmp", tag="ktmp")
             nc.scalar.activation(out=ktmp[:], in_=kv[:, :, 0, :], func=ACT.Identity, bias=bkc[:], scale=0.25)
-            qsb = stream.tile([P, n_g, O], F32, name="qsb", tag="qsb")
+            state[("ktmp", gi)] = ktmp
+
+        def keys_odd(gi):
+            rows = group_rows(gi)
+            r_a = row0[K_GROUPS[gi][0]]
+            kv = state[("kps", gi)][:, 0 : rows * 32].rearrange("p (m e n) -> p m e n", e=2, n=32)
+            ksb = outs.tile([P, rows // 2, 32], F32, name="ksb", tag="ksb")
+            nc.vector.scalar_tensor_tensor(
+                out=ksb[:], in0=kv[:, :, 1, :], scalar=0.25, in1=state[("ktmp", gi)][:], op0=ALU.mult, op1=ALU.add
+            )
+            nc.sync.dma_start(out=k2[:, r_a * 16 : (r_a + rows) * 16], in_=ksb[:].rearrange("p m n -> p (m n)"))
+
+        def queries_out(c):
+            rows = CHUNK_ROWS[c]
+            n_g = rows // 2
+            qsb = outs.tile([P, n_g, O], F32, name="qsb", tag="qsb")
             nc.vector.tensor_tensor(
                 out=qsb[:],
-                in0=qps[:, 0 : n_g * O].rearrange("p (g o) -> p g o", o=O),
+                in0=state[("qps", c)][:, 0 : n_g * O].rearrange("p (g o) -> p g o", o=O),
                 in1=state["bqb"][:].unsqueeze(1).to_broadcast([P, n_g, O]),
                 op=ALU.add,
             )
@@ -178,19 +242,22 @@ def tile_selfattention_pb_kernel(tc, x_bytes, x_scale, Wq, bq, Wk, bk, out_0, ou
                 out=q2[row0[c] * W : (row0[c] + rows) * W, :].rearrange("(i p d) o -> p i (d o)", p=P, d=2),
                 in_=qsb[:].rearrange("p (i d) o -> p i (d o)", d=2),
             )
-            ksb = stream.tile([P, n_m, 32], F32, name="ksb", tag="ksb")
-            nc.vector.scalar_tensor_tensor(out=ksb[:], in0=kv[:, :, 1, :], scalar=0.25, in1=ktmp[:], op0=ALU.mult, op1=ALU.add)
-            nc.sync.dma_start(
-                out=k2[:, row0[c] * 16 : (row0[c] + rows) * 16],
-                in_=ksb[:].rearrange("p m n -> p (m n)"),
-            )
 
-        widen(0)
-        for s in range(n_chunks + 2):
-            if s + 1 < n_chunks:
-                widen(s + 1)
+        for c in range(min(S_LEAD, n_chunks)):
+            widen(c, False)
+        widen(0, True)
+        interleave_gpsimd(0)
+        for s in range(n_chunks + K_LAG + 1):
+            c_k = s - K_LAG
+            last_of_group = 0 <= c_k < n_chunks and c_k == K_GROUPS[group_of[c_k]][-1]
+            if last_of_group:
+                keys_even(group_of[c_k])
+            if s + S_LEAD < n_chunks:
+                widen(s + S_LEAD, False)
             if s < n_chunks:
                 interleave(s)
+            if s + 1 < n_chunks:
+                widen(s + 1, True)
             if s == 0:
                 weights_a()
             if s == 1:
@@ -198,5 +265,9 @@ def tile_selfattention_pb_kernel(tc, x_bytes, x_scale, Wq, bq, Wk, bk, out_0, ou
             if 0 <= s - 1 < n_chunks:
                 quantize(s - 1)
                 multiply(s - 1)
+            if s + 1 < n_chunks:
+                interleave_gpsimd(s + 1)
             if 0 <= s - 2 < n_chunks:
-                finish(s - 2)
+                queries_out(s - 2)
+            if last_of_group:
+                keys_odd(group_of[c_k])

@@ -28,7 +28,7 @@ SCALAR_INTERLEAVES = {1: (1,), 7: (1,), 8: (1,)}
 GPSIMD_COLUMNS = {}
 S_LEAD = 2
 K_LAG = 2
-RUN = 1
+RUN = 4
 
 
 def tile_selfattention_pb_kernel(tc, x_bytes, x_scale, Wq, bq, Wk, bk, out_0, out_1):

@@ -23,8 +23,8 @@ FLOPS = 2 * 2 * O * C * T
 CHUNK_ROWS = [4, 8, 8, 8, 8, 8, 8, 8, 4]
 LOAD_ROWS = [4, 8, 8, 16, 28]
 K_GROUPS = [[0, 1], [2, 3], [4, 5], [6, 7], [8]]
-VECTOR_WIDENS = {0: (2, 3), 1: (2, 3), 2: (3,), 3: (3,), 4: (3,), 8: (3,)}
-SCALAR_INTERLEAVES = {1: (1,), 7: (1,), 8: (1,)}
+VECTOR_WIDENS = {0: (2, 3), 1: (3,), 2: (3,)}
+SCALAR_INTERLEAVES = {7: (1,), 8: (0, 1)}
 GPSIMD_COLUMNS = {}
 S_LEAD = 2
 K_LAG = 2

@@ -27,7 +27,7 @@ VECTOR_WIDENS = {0: (2, 3), 1: (3,), 2: (3,)}
 SCALAR_INTERLEAVES = {7: (1,), 8: (0, 1)}
 GPSIMD_COLUMNS = {}
 S_LEAD = 2
-K_LAG = 2
+K_LAG = 3
 RUN = 4
 
 

@@ -23,7 +23,7 @@ FLOPS = 2 * 2 * O * C * T
 CHUNK_ROWS = [4, 8, 8, 8, 8, 8, 8, 8, 4]
 LOAD_ROWS = [4, 8, 8, 16, 28]
 K_GROUPS = [[0, 1], [2, 3], [4, 5], [6, 7], [8]]
-VECTOR_WIDENS = {0: (2, 3), 1: (3,), 2: (3,)}
+VECTOR_WIDENS = {0: (2, 3), 1: (2, 3), 2: (3,)}
 SCALAR_INTERLEAVES = {7: (1,), 8: (0, 1)}
 GPSIMD_COLUMNS = {}
 S_LEAD = 2
@@ -146,23 +146,29 @@ def tile_selfattention_pb_kernel(tc, x_bytes, x_scale, Wq, bq, Wk, bk, out_0, ou
             nc.vector.quantize_mx(out=xc[:].bitcast(FP8X4), scales=xsc[:], in_=state[("xg", c)][:])
             state[("xc", c)] = (xc, xsc)
 
-        def weights_a():
+        def weights_tensor():
             wps = psum1.tile([P, 4 * P], F32, name="wps")
             words = wraw[:].bitcast(F32)
             for w in range(2):
                 for u in range(2):
                     nc.tensor.transpose(wps[:, (2 * w + u) * P : (2 * w + u + 1) * P], words[:, w, u : C // 2 : 2], ident[:])
+            state["wps"] = wps
+            bps = psum1.tile([P, O], F32, name="bps")
+            nc.tensor.matmul(bps[:], lhsT=ones[:], rhs=brow[:], start=True, stop=True)
+            state["bps"] = bps
+
+        def bias_out():
+            bqb = keep.tile([P, O], F32, name="bqb")
+            nc.scalar.copy(out=bqb[:], in_=state["bps"][:])
+            state["bqb"] = bqb
+
+        def weights_a():
             wg = keep.tile([P, 2 * O * 4], BF16, name="wg", align_bytes=64)
             nc.vector.tensor_copy(
                 out=wg[:].bitcast(F32).rearrange("p (w o u) -> p w o u", w=2, u=2),
-                in_=wps[:].rearrange("p (w u o) -> p w o u", w=2, u=2),
+                in_=state["wps"][:].rearrange("p (w u o) -> p w o u", w=2, u=2),
             )
             state["wg"] = wg
-            bps = psum1.tile([P, O], F32, name="bps")
-            nc.tensor.matmul(bps[:], lhsT=ones[:], rhs=brow[:], start=True, stop=True)
-            bqb = keep.tile([P, O], F32, name="bqb")
-            nc.scalar.copy(out=bqb[:], in_=bps[:])
-            state["bqb"] = bqb
 
         def weights_b():
             wc = keep.tile([P, 2 * O], U32, name="wc", align_bytes=64)
@@ -246,7 +252,9 @@ def tile_selfattention_pb_kernel(tc, x_bytes, x_scale, Wq, bq, Wk, bk, out_0, ou
         for c in range(min(S_LEAD, n_chunks)):
             widen(c, False)
         widen(0, True)
+        widen(1, True)
         interleave_gpsimd(0)
+        weights_tensor()
         for s in range(n_chunks + K_LAG + 1):
             c_k = s - K_LAG
             last_of_group = 0 <= c_k < n_chunks and c_k == K_GROUPS[group_of[c_k]][-1]
@@ -254,16 +262,19 @@ def tile_selfattention_pb_kernel(tc, x_bytes, x_scale, Wq, bq, Wk, bk, out_0, ou
                 keys_even(group_of[c_k])
             if s + S_LEAD < n_chunks:
                 widen(s + S_LEAD, False)
+            if s == 0:
+                bias_out()
             if s < n_chunks:
                 interleave(s)
-            if s + 1 < n_chunks:
-                widen(s + 1, True)
-            if s == 0:
+            if s == 1:
                 weights_a()
+            if 1 <= s and s + 1 < n_chunks:
+                widen(s + 1, True)
+            if 0 <= s - 1 < n_chunks:
+                quantize(s - 1)
             if s == 1:
                 weights_b()
             if 0 <= s - 1 < n_chunks:
-                quantize(s - 1)
                 multiply(s - 1)
             if s + 1 < n_chunks:
                 interleave_gpsimd(s + 1)

@@ -65,7 +65,7 @@ def tile_selfattention_pb_kernel(tc, x_bytes, x_scale, Wq, bq, Wk, bk, out_0, ou
             xbytes = keep.tile([P, 4, n_px], U8, name="xbytes%d" % d)
             nc.sync.dma_start(out=xbytes[:], in_=xv[:, :, load0[d] * W : load0[d] * W + n_px])
             xb.append(xbytes)
-            if d == 1:
+            if d == 2:
                 nc.sync.dma_start(out=wraw[:, 0, :], in_=Wq)
                 nc.sync.dma_start(out=wraw[:, 1, :], in_=Wk)
         warm = keep.tile([P, 1], F32, name="warm")
@@ -147,15 +147,15 @@ def tile_selfattention_pb_kernel(tc, x_bytes, x_scale, Wq, bq, Wk, bk, out_0, ou
             state[("xc", c)] = (xc, xsc)
 
         def weights_tensor():
+            bps = psum1.tile([P, O], F32, name="bps")
+            nc.tensor.matmul(bps[:], lhsT=ones[:], rhs=brow[:], start=True, stop=True)
+            state["bps"] = bps
             wps = psum1.tile([P, 4 * P], F32, name="wps")
             words = wraw[:].bitcast(F32)
             for w in range(2):
                 for u in range(2):
                     nc.tensor.transpose(wps[:, (2 * w + u) * P : (2 * w + u + 1) * P], words[:, w, u : C // 2 : 2], ident[:])
             state["wps"] = wps
-            bps = psum1.tile([P, O], F32, name="bps")
-            nc.tensor.matmul(bps[:], lhsT=ones[:], rhs=brow[:], start=True, stop=True)
-            state["bps"] = bps
 
         def bias_out():
             bqb = keep.tile([P, O], F32, name="bqb")
@@ -264,17 +264,18 @@ def tile_selfattention_pb_kernel(tc, x_bytes, x_scale, Wq, bq, Wk, bk, out_0, ou
                 widen(s + S_LEAD, False)
             if s == 0:
                 bias_out()
+            if s == 2:
+                weights_a()
             if s < n_chunks:
                 interleave(s)
-            if s == 1:
-                weights_a()
             if 1 <= s and s + 1 < n_chunks:
                 widen(s + 1, True)
+            if s == 2:
+                weights_b()
+                multiply(0)
             if 0 <= s - 1 < n_chunks:
                 quantize(s - 1)
-            if s == 1:
-                weights_b()
-            if 0 <= s - 1 < n_chunks:
+            if 1 <= s - 1 < n_chunks:
                 multiply(s - 1)
             if s + 1 < n_chunks:
                 interleave_gpsimd(s + 1)

@@ -279,7 +279,9 @@ def tile_selfattention_pb_kernel(tc, x_bytes, x_scale, Wq, bq, Wk, bk, out_0, ou
                 multiply(s - 1)
             if s + 1 < n_chunks:
                 interleave_gpsimd(s + 1)
-            if 0 <= s - 2 < n_chunks:
+            if s == 3:
+                queries_out(0)
+            if 1 <= s - 2 < n_chunks:
                 queries_out(s - 2)
             if last_of_group:
                 keys_odd(group_of[c_k])

@@ -28,7 +28,7 @@ SCALAR_INTERLEAVES = {7: (1,), 8: (0, 1)}
 GPSIMD_COLUMNS = {}
 S_LEAD = 2
 K_LAG = 3
-RUN = 4
+RUN = 8
 
 
 def tile_selfattention_pb_kernel(tc, x_bytes, x_scale, Wq, bq, Wk, bk, out_0, out_1):

@@ -23,7 +23,7 @@ FLOPS = 2 * 2 * O * C * T
 CHUNK_ROWS = [4, 8, 8, 8, 8, 8, 8, 8, 4]
 LOAD_ROWS = [4, 8, 8, 16, 28]
 K_GROUPS = [[0, 1], [2, 3], [4, 5], [6, 7], [8]]
-VECTOR_WIDENS = {0: (2, 3), 1: (2, 3), 2: (3,)}
+VECTOR_WIDENS = {0: (2, 3), 1: (2, 3), 2: (3,), 3: (3,)}
 SCALAR_INTERLEAVES = {7: (1,), 8: (0, 1)}
 GPSIMD_COLUMNS = {}
 S_LEAD = 2
@@ -164,7 +164,7 @@ def tile_selfattention_pb_kernel(tc, x_bytes, x_scale, Wq, bq, Wk, bk, out_0, ou
 
         def weights_a():
             wg = keep.tile([P, 2 * O * 4], BF16, name="wg", align_bytes=64)
-            nc.vector.tensor_copy(
+            nc.scalar.copy(
                 out=wg[:].bitcast(F32).rearrange("p (w o u) -> p w o u", w=2, u=2),
                 in_=state["wps"][:].rearrange("p (w u o) -> p w o u", w=2, u=2),
             )
@@ -264,12 +264,11 @@ def tile_selfattention_pb_kernel(tc, x_bytes, x_scale, Wq, bq, Wk, bk, out_0, ou
                 widen(s + S_LEAD, False)
             if s == 0:
                 bias_out()
-            if s == 2:
                 weights_a()
-            if s < n_chunks:
-                interleave(s)
             if 1 <= s and s + 1 < n_chunks:
                 widen(s + 1, True)
+            if s < n_chunks:
+                interleave(s)
             if s == 2:
                 weights_b()
                 multiply(0)

@@ -7,6 +7,7 @@ F32 = mybir.dt.float32
 BF16 = mybir.dt.bfloat16
 U32 = mybir.dt.uint32
 U8 = mybir.dt.uint8
+I32 = mybir.dt.int32
 FP8 = mybir.dt.float8_e4m3fn
 FP8X4 = mybir.dt.float8_e4m3fn_x4
 ACT = mybir.ActivationFunctionType
@@ -29,6 +30,9 @@ GPSIMD_COLUMNS = {}
 S_LEAD = 2
 K_LAG = 3
 RUN = 8
+PITCH = 576
+SHIFTED_GROUPS = 3
+SHIFT_LAG = 3
 
 
 def tile_selfattention_pb_kernel(tc, x_bytes, x_scale, Wq, bq, Wk, bk, out_0, out_1):
@@ -49,7 +53,6 @@ def tile_selfattention_pb_kernel(tc, x_bytes, x_scale, Wq, bq, Wk, bk, out_0, ou
         keep = ctx.enter_context(tc.tile_pool(name="keep", bufs=1))
         planes = ctx.enter_context(tc.tile_pool(name="planes", bufs=4))
         grouped = ctx.enter_context(tc.tile_pool(name="grouped", bufs=3))
-        codes = ctx.enter_context(tc.tile_pool(name="codes", bufs=3))
         outs = ctx.enter_context(tc.tile_pool(name="outs", bufs=4))
         psum1 = ctx.enter_context(tc.psum_pool(name="psum1", bufs=1))
         psumq = ctx.enter_context(tc.psum_pool(name="psumq", bufs=4))
@@ -81,6 +84,14 @@ def tile_selfattention_pb_kernel(tc, x_bytes, x_scale, Wq, bq, Wk, bk, out_0, ou
         make_identity(nc, ident[:])
         ones = keep.tile([P, P], BF16, name="ones")
         nc.gpsimd.memset(ones[:], 1.0)
+        xc_all = keep.tile([P, n_chunks, PITCH], U32, name="xc_all", align_bytes=64)
+        xsc_all = keep.tile([P, n_chunks, PITCH], U8, name="xsc_all", align_bytes=64)
+        xsh_all = keep.tile([P, n_chunks, PITCH], U8, name="xsh_all", align_bytes=64)
+        n_shift = K_GROUPS[SHIFTED_GROUPS - 1][-1] + 1
+        nc.gpsimd.memset(xsc_all[:, 0:n_shift, :].bitcast(I32), 0)
+        for c in range(n_shift):
+            n_px = CHUNK_ROWS[c] * W
+            nc.gpsimd.memset(xc_all[:, c, n_px : n_px + 32].bitcast(I32), 0)
 
         state = {}
 
@@ -141,10 +152,9 @@ def tile_selfattention_pb_kernel(tc, x_bytes, x_scale, Wq, bq, Wk, bk, out_0, ou
 
         def quantize(c):
             n_px = CHUNK_ROWS[c] * W
-            xc = codes.tile([P, n_px], U32, name="xc", tag="xc", align_bytes=64)
-            xsc = codes.tile([P, n_px], U8, name="xsc", tag="xsc", align_bytes=64)
-            nc.vector.quantize_mx(out=xc[:].bitcast(FP8X4), scales=xsc[:], in_=state[("xg", c)][:])
-            state[("xc", c)] = (xc, xsc)
+            nc.vector.quantize_mx(out=xc_all[:, c, 0:n_px].bitcast(FP8X4), scales=xsc_all[:, c, 0:n_px], in_=state[("xg", c)][:])
+            if group_of[c] < SHIFTED_GROUPS:
+                nc.sync.dma_start(out=xsh_all[:, c, 0:n_px].bitcast(I32), in_=xsc_all[:, c, 32 : 32 + n_px].bitcast(I32))
 
         def weights_tensor():
             bps = psum1.tile([P, O], F32, name="bps")
@@ -178,7 +188,8 @@ def tile_selfattention_pb_kernel(tc, x_bytes, x_scale, Wq, bq, Wk, bk, out_0, ou
 
         def multiply(c):
             rows = CHUNK_ROWS[c]
-            xc, xsc = state[("xc", c)]
+            xc = xc_all[:, c, :]
+            xsc = xsc_all[:, c, :]
             wc, wsc = state["wc"]
             n_ih = rows // 4
             qps = psumq.tile([P, 4 * O], F32, name="qps", tag="qps")
@@ -195,6 +206,16 @@ def tile_selfattention_pb_kernel(tc, x_bytes, x_scale, Wq, bq, Wk, bk, out_0, ou
                         start=True,
                         stop=True,
                     )
+            state[("qps", c)] = qps
+            if group_of[c] >= SHIFTED_GROUPS:
+                multiply_keys(c)
+
+        def multiply_keys(c):
+            rows = CHUNK_ROWS[c]
+            xc = xc_all[:, c, :]
+            xsc = xsc_all[:, c, :]
+            xsh = xsh_all[:, c, :]
+            wc, wsc = state["wc"]
             gi = group_of[c]
             if c == K_GROUPS[gi][0]:
                 kps_new = psumk.tile([P, 512], F32, name="kps", tag="kps")
@@ -202,17 +223,23 @@ def tile_selfattention_pb_kernel(tc, x_bytes, x_scale, Wq, bq, Wk, bk, out_0, ou
             kps = state[("kps", gi)]
             k0 = (row0[c] - row0[K_GROUPS[gi][0]]) * 32
             n_k = rows * 32
+            windows = []
             for dj in range(2):
+                windows.append((dj * n_k, xsc))
+                if gi < SHIFTED_GROUPS:
+                    windows.append((dj * n_k + 32, xsh))
+            for i in range(len(windows)):
+                at, scales = windows[i]
+                s_at = at // 64 * 64
                 nc.tensor.matmul_mx(
                     out=kps[:, k0 : k0 + n_k],
                     lhsT=wc[:, O : 2 * O].bitcast(FP8X4),
                     lhsT_scale=wsc[:, O : 2 * O],
-                    rhs=xc[:, dj * n_k : (dj + 1) * n_k].bitcast(FP8X4),
-                    rhs_scale=xsc[:, dj * n_k : (dj + 1) * n_k],
-                    start=(dj == 0),
-                    stop=(dj == 1),
+                    rhs=xc[:, at : at + n_k].bitcast(FP8X4),
+                    rhs_scale=scales[:, s_at : s_at + n_k],
+                    start=(i == 0),
+                    stop=(i == len(windows) - 1),
                 )
-            state[("qps", c)] = qps
 
         def group_rows(gi):
             return sum(CHUNK_ROWS[c] for c in K_GROUPS[gi])
@@ -223,6 +250,14 @@ def tile_selfattention_pb_kernel(tc, x_bytes, x_scale, Wq, bq, Wk, bk, out_0, ou
             ktmp = outs.tile([P, rows // 2, 32], F32, name="ktmp", tag="ktmp")
             nc.scalar.activation(out=ktmp[:], in_=kv[:, :, 0, :], func=ACT.Identity, bias=bkc[:], scale=0.25)
             state[("ktmp", gi)] = ktmp
+
+        def keys_whole(gi):
+            rows = group_rows(gi)
+            r_a = row0[K_GROUPS[gi][0]]
+            kv = state[("kps", gi)][:, 0 : rows * 32].rearrange("p (m e n) -> p m e n", e=2, n=32)
+            ksb = outs.tile([P, rows // 2, 32], F32, name="ksb", tag="ksb")
+            nc.scalar.activation(out=ksb[:], in_=kv[:, :, 0, :], func=ACT.Identity, bias=bkc[:], scale=0.25)
+            nc.sync.dma_start(out=k2[:, r_a * 16 : (r_a + rows) * 16], in_=ksb[:].rearrange("p m n -> p (m n)"))
 
         def keys_odd(gi):
             rows = group_rows(gi)
@@ -257,7 +292,10 @@ def tile_selfattention_pb_kernel(tc, x_bytes, x_scale, Wq, bq, Wk, bk, out_0, ou
         weights_tensor()
         for s in range(n_chunks + K_LAG + 1):
             c_k = s - K_LAG
-            last_of_group = 0 <= c_k < n_chunks and c_k == K_GROUPS[group_of[c_k]][-1]
+            last_of_group = 0 <= c_k < n_chunks and c_k == K_GROUPS[group_of[c_k]][-1] and group_of[c_k] >= SHIFTED_GROUPS
+            c_w = s - SHIFT_LAG - 1
+            if 0 <= c_w < n_chunks and c_w == K_GROUPS[group_of[c_w]][-1] and group_of[c_w] < SHIFTED_GROUPS:
+                keys_whole(group_of[c_w])
             if last_of_group:
                 keys_even(group_of[c_k])
             if s + S_LEAD < n_chunks:
@@ -274,6 +312,8 @@ def tile_selfattention_pb_kernel(tc, x_bytes, x_scale, Wq, bq, Wk, bk, out_0, ou
                 multiply(0)
             if 0 <= s - 1 < n_chunks:
                 quantize(s - 1)
+            if 0 <= s - SHIFT_LAG < n_chunks and group_of[s - SHIFT_LAG] < SHIFTED_GROUPS:
+                multiply_keys(s - SHIFT_LAG)
             if 1 <= s - 1 < n_chunks:
                 multiply(s - 1)
             if s + 1 < n_chunks:

@@ -26,7 +26,6 @@ LOAD_ROWS = [4, 8, 8, 16, 28]
 K_GROUPS = [[0, 1], [2, 3], [4, 5], [6, 7], [8]]
 VECTOR_WIDENS = {0: (2, 3), 1: (2, 3), 2: (3,), 3: (3,)}
 SCALAR_INTERLEAVES = {7: (1,), 8: (0, 1)}
-GPSIMD_COLUMNS = {}
 S_LEAD = 2
 K_LAG = 3
 RUN = 8
@@ -116,39 +115,29 @@ def tile_selfattention_pb_kernel(tc, x_bytes, x_scale, Wq, bq, Wk, bk, out_0, ou
         def views(c):
             xw = state[("xw", c)]
             xg = state[("xg", c)]
-            if RUN == 1:
-                dst = xg[:].rearrange("p (d c t) -> p d c t", d=2, t=4)
-                src = xw[:].rearrange("p t (c d) -> p d c t", d=2)
-            else:
-                dst = xg[:].rearrange("p (d c i t) -> p d c t i", d=2, t=4, i=RUN)
-                src = xw[:].rearrange("p t (c i d) -> p d c t i", d=2, i=RUN)
+            if RUN > 1:
+                dst = xg[:].rearrange("p (d c i t) -> p c d t i", d=2, t=4, i=RUN)
+                src = xw[:].rearrange("p t (c i d) -> p c d t i", d=2, i=RUN)
             return dst, src
 
         def interleave_gpsimd(c):
             n_px = CHUNK_ROWS[c] * W
             xg_new = grouped.tile([P, 4 * n_px], BF16, name="xg", tag="xg", align_bytes=64)
             state[("xg", c)] = xg_new
-            g = GPSIMD_COLUMNS.get(c, 0) // RUN
-            if g > 0:
-                dst, src = views(c)
-                n_c = n_px // 2 // RUN
-                nc.gpsimd.tensor_scalar(
-                    out=dst[:, :, n_c - g : n_c], in0=src[:, :, n_c - g : n_c], scalar1=1.0, scalar2=0.0, op0=ALU.mult, op1=ALU.add
-                )
 
         def interleave(c):
             n_px = CHUNK_ROWS[c] * W
             dst, src = views(c)
-            n_c = n_px // 2 // RUN - GPSIMD_COLUMNS.get(c, 0) // RUN
+            n_c = n_px // 2 // RUN
             on_scalar = SCALAR_INTERLEAVES.get(c, ())
             if len(on_scalar) == 0:
-                nc.vector.tensor_copy(out=dst[:, :, 0:n_c], in_=src[:, :, 0:n_c])
+                nc.vector.tensor_copy(out=dst[:, 0:n_c], in_=src[:, 0:n_c])
             else:
                 for d in range(2):
                     if d in on_scalar:
-                        nc.scalar.copy(out=dst[:, d, 0:n_c], in_=src[:, d, 0:n_c])
+                        nc.scalar.copy(out=dst[:, 0:n_c, d], in_=src[:, 0:n_c, d])
                     else:
-                        nc.vector.tensor_copy(out=dst[:, d, 0:n_c], in_=src[:, d, 0:n_c])
+                        nc.vector.tensor_copy(out=dst[:, 0:n_c, d], in_=src[:, 0:n_c, d])
 
         def quantize(c):
             n_px = CHUNK_ROWS[c] * W

@@ -22,7 +22,7 @@ T = H * W
 FLOPS = 2 * 2 * O * C * T
 
 CHUNK_ROWS = [4, 8, 8, 8, 8, 8, 8, 8, 4]
-LOAD_ROWS = [4, 8, 8, 16, 28]
+LOAD_ROWS = [4, 8, 8, 16, 16, 12]
 K_GROUPS = [[0, 1], [2, 3], [4, 5], [6, 7], [8]]
 VECTOR_WIDENS = {0: (2, 3), 1: (2, 3), 2: (3,), 3: (3,)}
 SCALAR_INTERLEAVES = {7: (1,), 8: (0, 1)}
@@ -60,6 +60,13 @@ def tile_selfattention_pb_kernel(tc, x_bytes, x_scale, Wq, bq, Wk, bk, out_0, ou
 
         xs = keep.tile([P, 4], F32, name="xs")
         nc.scalar.dma_start(out=xs[:], in_=x_scale.rearrange("a (p t) b c -> p (a t b c)", t=4))
+        warm = keep.tile([P, 1], F32, name="warm")
+        nc.gpsimd.memset(warm[:], 0.0)
+        brow = keep.tile([P, O], BF16, name="brow")
+        nc.gpsimd.memset(brow[:], 0.0)
+        warm2 = keep.tile([P, 1], F32, name="warm2")
+        nc.scalar.activation(out=warm2[:], in_=warm[:], func=ACT.Copy)
+        bkc = keep.tile([P, 1], BF16, name="bkc")
         xb = []
         wraw = keep.tile([P, 2, C], BF16, name="wraw")
         for d in range(len(LOAD_ROWS)):
@@ -70,15 +77,8 @@ def tile_selfattention_pb_kernel(tc, x_bytes, x_scale, Wq, bq, Wk, bk, out_0, ou
             if d == 2:
                 nc.sync.dma_start(out=wraw[:, 0, :], in_=Wq)
                 nc.sync.dma_start(out=wraw[:, 1, :], in_=Wk)
-        warm = keep.tile([P, 1], F32, name="warm")
-        nc.gpsimd.memset(warm[:], 0.0)
-        brow = keep.tile([P, O], BF16, name="brow")
-        nc.gpsimd.memset(brow[:], 0.0)
-        warm2 = keep.tile([P, 1], F32, name="warm2")
-        nc.scalar.activation(out=warm2[:], in_=warm[:], func=ACT.Copy)
-        nc.scalar.dma_start(out=brow[0:1, :], in_=bq.rearrange("(a o) -> a o", a=1))
-        bkc = keep.tile([P, 1], BF16, name="bkc")
-        nc.scalar.dma_start(out=bkc[:], in_=bk.rearrange("(p a) -> p a", a=1))
+                nc.scalar.dma_start(out=brow[0:1, :], in_=bq.rearrange("(a o) -> a o", a=1))
+                nc.scalar.dma_start(out=bkc[:], in_=bk.rearrange("(p a) -> p a", a=1))
         ident = keep.tile([P, P], F32, name="ident")
         make_identity(nc, ident[:])
         ones = keep.tile([P, P], BF16, name="ones")

@@ -22,9 +22,9 @@ T = H * W
 FLOPS = 2 * 2 * O * C * T
 
 CHUNK_ROWS = [4, 8, 8, 8, 8, 8, 8, 8, 4]
-LOAD_ROWS = [4, 8, 8, 16, 16, 12]
+LOAD_ROWS = [4, 8, 8, 8, 8, 16, 12]
 K_GROUPS = [[0, 1], [2, 3], [4, 5], [6, 7], [8]]
-VECTOR_WIDENS = {0: (2, 3), 1: (2, 3), 2: (3,), 3: (3,)}
+VECTOR_WIDENS = {0: (2, 3), 1: (2, 3), 2: (2, 3), 3: (3,)}
 SCALAR_INTERLEAVES = {7: (1,), 8: (0, 1)}
 S_LEAD = 2
 K_LAG = 3
@@ -74,7 +74,7 @@ def tile_selfattention_pb_kernel(tc, x_bytes, x_scale, Wq, bq, Wk, bk, out_0, ou
             xbytes = keep.tile([P, 4, n_px], U8, name="xbytes%d" % d)
             nc.sync.dma_start(out=xbytes[:], in_=xv[:, :, load0[d] * W : load0[d] * W + n_px])
             xb.append(xbytes)
-            if d == 2:
+            if d == 3:
                 nc.sync.dma_start(out=wraw[:, 0, :], in_=Wq)
                 nc.sync.dma_start(out=wraw[:, 1, :], in_=Wk)
                 nc.scalar.dma_start(out=brow[0:1, :], in_=bq.rearrange("(a o) -> a o", a=1))
@@ -291,16 +291,17 @@ def tile_selfattention_pb_kernel(tc, x_bytes, x_scale, Wq, bq, Wk, bk, out_0, ou
                 widen(s + S_LEAD, False)
             if s == 0:
                 bias_out()
+            if s == 1:
                 weights_a()
             if 1 <= s and s + 1 < n_chunks:
                 widen(s + 1, True)
             if s < n_chunks:
                 interleave(s)
+            if 0 <= s - 1 < n_chunks:
+                quantize(s - 1)
             if s == 2:
                 weights_b()
                 multiply(0)
-            if 0 <= s - 1 < n_chunks:
-                quantize(s - 1)
             if 0 <= s - SHIFT_LAG < n_chunks and group_of[s - SHIFT_LAG] < SHIFTED_GROUPS:
                 multiply_keys(s - SHIFT_LAG)
             if 1 <= s - 1 < n_chunks:

from contextlib import ExitStack

import concourse.mybir as mybir
from concourse.masks import make_identity

F32 = mybir.dt.float32
BF16 = mybir.dt.bfloat16
U32 = mybir.dt.uint32
U8 = mybir.dt.uint8
I32 = mybir.dt.int32
FP8 = mybir.dt.float8_e4m3fn
FP8X4 = mybir.dt.float8_e4m3fn_x4
ACT = mybir.ActivationFunctionType
ALU = mybir.AluOpType

P = 128
C = 512
O = 128
H = 64
W = 64
T = H * W
FLOPS = 2 * 2 * O * C * T

CHUNK_ROWS = [4, 8, 8, 8, 8, 8, 8, 8, 4]
LOAD_ROWS = [4, 8, 8, 8, 8, 16, 12]
K_GROUPS = [[0, 1], [2, 3], [4, 5], [6, 7], [8]]
VECTOR_WIDENS = {0: (2, 3), 1: (2, 3), 2: (2, 3), 3: (3,)}
SCALAR_INTERLEAVES = {7: (1,), 8: (0, 1)}
S_LEAD = 2
K_LAG = 3
RUN = 8
PITCH = 576
SHIFTED_GROUPS = 3
SHIFT_LAG = 3


def tile_selfattention_pb_kernel(tc, x_bytes, x_scale, Wq, bq, Wk, bk, out_0, out_1):
    nc = tc.nc
    n_chunks = len(CHUNK_ROWS)
    row0 = [sum(CHUNK_ROWS[:c]) for c in range(n_chunks)]
    load0 = [sum(LOAD_ROWS[:d]) for d in range(len(LOAD_ROWS))]
    group_of = {}
    for gi in range(len(K_GROUPS)):
        for c in K_GROUPS[gi]:
            group_of[c] = gi

    xv = x_bytes.rearrange("b (p t) h w -> p t (b h w)", t=4)
    q2 = out_0.rearrange("b n o -> (b n) o")
    k2 = out_1.rearrange("b o n -> (b o) n")

    with ExitStack() as ctx:
        keep = ctx.enter_context(tc.tile_pool(name="keep", bufs=1))
        planes = ctx.enter_context(tc.tile_pool(name="planes", bufs=4))
        grouped = ctx.enter_context(tc.tile_pool(name="grouped", bufs=3))
        outs = ctx.enter_context(tc.tile_pool(name="outs", bufs=4))
        psum1 = ctx.enter_context(tc.psum_pool(name="psum1", bufs=1))
        psumq = ctx.enter_context(tc.psum_pool(name="psumq", bufs=4))
        psumk = ctx.enter_context(tc.psum_pool(name="psumk", bufs=2))
        ctx.enter_context(tc.manual_schedule())

        xs = keep.tile([P, 4], F32, name="xs")
        nc.scalar.dma_start(out=xs[:], in_=x_scale.rearrange("a (p t) b c -> p (a t b c)", t=4))
        warm = keep.tile([P, 1], F32, name="warm")
        nc.gpsimd.memset(warm[:], 0.0)
        brow = keep.tile([P, O], BF16, name="brow")
        nc.gpsimd.memset(brow[:], 0.0)
        warm2 = keep.tile([P, 1], F32, name="warm2")
        nc.scalar.activation(out=warm2[:], in_=warm[:], func=ACT.Copy)
        bkc = keep.tile([P, 1], BF16, name="bkc")
        xb = []
        wraw = keep.tile([P, 2, C], BF16, name="wraw")
        for d in range(len(LOAD_ROWS)):
            n_px = LOAD_ROWS[d] * W
            xbytes = keep.tile([P, 4, n_px], U8, name="xbytes%d" % d)
            nc.sync.dma_start(out=xbytes[:], in_=xv[:, :, load0[d] * W : load0[d] * W + n_px])
            xb.append(xbytes)
            if d == 3:
                nc.sync.dma_start(out=wraw[:, 0, :], in_=Wq)
                nc.sync.dma_start(out=wraw[:, 1, :], in_=Wk)
                nc.scalar.dma_start(out=brow[0:1, :], in_=bq.rearrange("(a o) -> a o", a=1))
                nc.scalar.dma_start(out=bkc[:], in_=bk.rearrange("(p a) -> p a", a=1))
        ident = keep.tile([P, P], F32, name="ident")
        make_identity(nc, ident[:])
        ones = keep.tile([P, P], BF16, name="ones")
        nc.gpsimd.memset(ones[:], 1.0)
        xc_all = keep.tile([P, n_chunks, PITCH], U32, name="xc_all", align_bytes=64)
        xsc_all = keep.tile([P, n_chunks, PITCH], U8, name="xsc_all", align_bytes=64)
        xsh_all = keep.tile([P, n_chunks, PITCH], U8, name="xsh_all", align_bytes=64)
        n_shift = K_GROUPS[SHIFTED_GROUPS - 1][-1] + 1
        nc.gpsimd.memset(xsc_all[:, 0:n_shift, :].bitcast(I32), 0)
        for c in range(n_shift):
            n_px = CHUNK_ROWS[c] * W
            nc.gpsimd.memset(xc_all[:, c, n_px : n_px + 32].bitcast(I32), 0)

        state = {}

        def widen(c, on_vector):
            rows = CHUNK_ROWS[c]
            n_px = rows * W
            d = max(i for i in range(len(LOAD_ROWS)) if load0[i] <= row0[c])
            off = (row0[c] - load0[d]) * W
            assert off + n_px <= LOAD_ROWS[d] * W
            if ("xw", c) not in state:
                xw_new = planes.tile([P, 4, n_px], BF16, name="xw", tag="xw")
                state[("xw", c)] = xw_new
            xw = state[("xw", c)]
            for t in range(4):
                src = xb[d][:, t, off : off + n_px].bitcast(FP8)
                if t in VECTOR_WIDENS.get(c, ()):
                    if on_vector:
                        nc.vector.tensor_scalar(out=xw[:, t, :], in0=src, scalar1=xs[:, t : t + 1], scalar2=None, op0=ALU.mult)
                elif not on_vector:
                    nc.scalar.activation(out=xw[:, t, :], in_=src, func=ACT.Copy, scale=xs[:, t : t + 1])

        def views(c):
            xw = state[("xw", c)]
            xg = state[("xg", c)]
            if RUN > 1:
                dst = xg[:].rearrange("p (d c i t) -> p c d t i", d=2, t=4, i=RUN)
                src = xw[:].rearrange("p t (c i d) -> p c d t i", d=2, i=RUN)
            return dst, src

        def interleave_gpsimd(c):
            n_px = CHUNK_ROWS[c] * W
            xg_new = grouped.tile([P, 4 * n_px], BF16, name="xg", tag="xg", align_bytes=64)
            state[("xg", c)] = xg_new

        def interleave(c):
            n_px = CHUNK_ROWS[c] * W
            dst, src = views(c)
            n_c = n_px // 2 // RUN
            on_scalar = SCALAR_INTERLEAVES.get(c, ())
            if len(on_scalar) == 0:
                nc.vector.tensor_copy(out=dst[:, 0:n_c], in_=src[:, 0:n_c])
            else:
                for d in range(2):
                    if d in on_scalar:
                        nc.scalar.copy(out=dst[:, 0:n_c, d], in_=src[:, 0:n_c, d])
                    else:
                        nc.vector.tensor_copy(out=dst[:, 0:n_c, d], in_=src[:, 0:n_c, d])

        def quantize(c):
            n_px = CHUNK_ROWS[c] * W
            nc.vector.quantize_mx(out=xc_all[:, c, 0:n_px].bitcast(FP8X4), scales=xsc_all[:, c, 0:n_px], in_=state[("xg", c)][:])
            if group_of[c] < SHIFTED_GROUPS:
                nc.sync.dma_start(out=xsh_all[:, c, 0:n_px].bitcast(I32), in_=xsc_all[:, c, 32 : 32 + n_px].bitcast(I32))

        def weights_tensor():
            bps = psum1.tile([P, O], F32, name="bps")
            nc.tensor.matmul(bps[:], lhsT=ones[:], rhs=brow[:], start=True, stop=True)
            state["bps"] = bps
            wps = psum1.tile([P, 4 * P], F32, name="wps")
            words = wraw[:].bitcast(F32)
            for w in range(2):
                for u in range(2):
                    nc.tensor.transpose(wps[:, (2 * w + u) * P : (2 * w + u + 1) * P], words[:, w, u : C // 2 : 2], ident[:])
            state["wps"] = wps

        def bias_out():
            bqb = keep.tile([P, O], F32, name="bqb")
            nc.scalar.copy(out=bqb[:], in_=state["bps"][:])
            state["bqb"] = bqb

        def weights_a():
            wg = keep.tile([P, 2 * O * 4], BF16, name="wg", align_bytes=64)
            nc.scalar.copy(
                out=wg[:].bitcast(F32).rearrange("p (w o u) -> p w o u", w=2, u=2),
                in_=state["wps"][:].rearrange("p (w u o) -> p w o u", w=2, u=2),
            )
            state["wg"] = wg

        def weights_b():
            wc = keep.tile([P, 2 * O], U32, name="wc", align_bytes=64)
            wsc = keep.tile([P, 2 * O], U8, name="wsc", align_bytes=64)
            nc.vector.quantize_mx(out=wc[:].bitcast(FP8X4), scales=wsc[:], in_=state["wg"][:])
            state["wc"] = (wc, wsc)

        def multiply(c):
            rows = CHUNK_ROWS[c]
            xc = xc_all[:, c, :]
            xsc = xsc_all[:, c, :]
            wc, wsc = state["wc"]
            n_ih = rows // 4
            qps = psumq.tile([P, 4 * O], F32, name="qps", tag="qps")
            for ih in range(n_ih):
                for dj in range(2):
                    g = dj * n_ih + ih
                    slot = ih * 2 + dj
                    nc.tensor.matmul_mx(
                        out=qps[:, slot * O : (slot + 1) * O],
                        lhsT=xc[:, g * P : (g + 1) * P].bitcast(FP8X4),
                        lhsT_scale=xsc[:, g * P : (g + 1) * P],
                        rhs=wc[:, 0:O].bitcast(FP8X4),
                        rhs_scale=wsc[:, 0:O],
                        start=True,
                        stop=True,
                    )
            state[("qps", c)] = qps
            if group_of[c] >= SHIFTED_GROUPS:
                multiply_keys(c)

        def multiply_keys(c):
            rows = CHUNK_ROWS[c]
            xc = xc_all[:, c, :]
            xsc = xsc_all[:, c, :]
            xsh = xsh_all[:, c, :]
            wc, wsc = state["wc"]
            gi = group_of[c]
            if c == K_GROUPS[gi][0]:
                kps_new = psumk.tile([P, 512], F32, name="kps", tag="kps")
                state[("kps", gi)] = kps_new
            kps = state[("kps", gi)]
            k0 = (row0[c] - row0[K_GROUPS[gi][0]]) * 32
            n_k = rows * 32
            windows = []
            for dj in range(2):
                windows.append((dj * n_k, xsc))
                if gi < SHIFTED_GROUPS:
                    windows.append((dj * n_k + 32, xsh))
            for i in range(len(windows)):
                at, scales = windows[i]
                s_at = at // 64 * 64
                nc.tensor.matmul_mx(
                    out=kps[:, k0 : k0 + n_k],
                    lhsT=wc[:, O : 2 * O].bitcast(FP8X4),
                    lhsT_scale=wsc[:, O : 2 * O],
                    rhs=xc[:, at : at + n_k].bitcast(FP8X4),
                    rhs_scale=scales[:, s_at : s_at + n_k],
                    start=(i == 0),
                    stop=(i == len(windows) - 1),
                )

        def group_rows(gi):
            return sum(CHUNK_ROWS[c] for c in K_GROUPS[gi])

        def keys_even(gi):
            rows = group_rows(gi)
            kv = state[("kps", gi)][:, 0 : rows * 32].rearrange("p (m e n) -> p m e n", e=2, n=32)
            ktmp = outs.tile([P, rows // 2, 32], F32, name="ktmp", tag="ktmp")
            nc.scalar.activation(out=ktmp[:], in_=kv[:, :, 0, :], func=ACT.Identity, bias=bkc[:], scale=0.25)
            state[("ktmp", gi)] = ktmp

        def keys_whole(gi):
            rows = group_rows(gi)
            r_a = row0[K_GROUPS[gi][0]]
            kv = state[("kps", gi)][:, 0 : rows * 32].rearrange("p (m e n) -> p m e n", e=2, n=32)
            ksb = outs.tile([P, rows // 2, 32], F32, name="ksb", tag="ksb")
            nc.scalar.activation(out=ksb[:], in_=kv[:, :, 0, :], func=ACT.Identity, bias=bkc[:], scale=0.25)
            nc.sync.dma_start(out=k2[:, r_a * 16 : (r_a + rows) * 16], in_=ksb[:].rearrange("p m n -> p (m n)"))

        def keys_odd(gi):
            rows = group_rows(gi)
            r_a = row0[K_GROUPS[gi][0]]
            kv = state[("kps", gi)][:, 0 : rows * 32].rearrange("p (m e n) -> p m e n", e=2, n=32)
            ksb = outs.tile([P, rows // 2, 32], F32, name="ksb", tag="ksb")
            nc.vector.scalar_tensor_tensor(
                out=ksb[:], in0=kv[:, :, 1, :], scalar=0.25, in1=state[("ktmp", gi)][:], op0=ALU.mult, op1=ALU.add
            )
            nc.sync.dma_start(out=k2[:, r_a * 16 : (r_a + rows) * 16], in_=ksb[:].rearrange("p m n -> p (m n)"))

        def queries_out(c):
            rows = CHUNK_ROWS[c]
            n_g = rows // 2
            qsb = outs.tile([P, n_g, O], F32, name="qsb", tag="qsb")
            nc.vector.tensor_tensor(
                out=qsb[:],
                in0=state[("qps", c)][:, 0 : n_g * O].rearrange("p (g o) -> p g o", o=O),
                in1=state["bqb"][:].unsqueeze(1).to_broadcast([P, n_g, O]),
                op=ALU.add,
            )
            nc.sync.dma_start(
                out=q2[row0[c] * W : (row0[c] + rows) * W, :].rearrange("(i p d) o -> p i (d o)", p=P, d=2),
                in_=qsb[:].rearrange("p (i d) o -> p i (d o)", d=2),
            )

        for c in range(min(S_LEAD, n_chunks)):
            widen(c, False)
        widen(0, True)
        widen(1, True)
        interleave_gpsimd(0)
        weights_tensor()
        for s in range(n_chunks + K_LAG + 1):
            c_k = s - K_LAG
            last_of_group = 0 <= c_k < n_chunks and c_k == K_GROUPS[group_of[c_k]][-1] and group_of[c_k] >= SHIFTED_GROUPS
            c_w = s - SHIFT_LAG - 1
            if 0 <= c_w < n_chunks and c_w == K_GROUPS[group_of[c_w]][-1] and group_of[c_w] < SHIFTED_GROUPS:
                keys_whole(group_of[c_w])
            if last_of_group:
                keys_even(group_of[c_k])
            if s + S_LEAD < n_chunks:
                widen(s + S_LEAD, False)
            if s == 0:
                bias_out()
            if s == 1:
                weights_a()
            if 1 <= s and s + 1 < n_chunks:
                widen(s + 1, True)
            if s < n_chunks:
                interleave(s)
            if 0 <= s - 1 < n_chunks:
                quantize(s - 1)
            if s == 2:
                weights_b()
                multiply(0)
            if 0 <= s - SHIFT_LAG < n_chunks and group_of[s - SHIFT_LAG] < SHIFTED_GROUPS:
                multiply_keys(s - SHIFT_LAG)
            if 1 <= s - 1 < n_chunks:
                multiply(s - 1)
            if s + 1 < n_chunks:
                interleave_gpsimd(s + 1)
            if s == 3:
                queries_out(0)
            if 1 <= s - 2 < n_chunks:
                queries_out(s - 2)
            if last_of_group:
                keys_odd(group_of[c_k])
